import numpy as np
import ml_dtypes


def mxq(x, axis, fmt="e4m3"):
    dtype, down = {"e4m3": (ml_dtypes.float8_e4m3fn, 7), "e5m2": (ml_dtypes.float8_e5m2, 14)}[fmt]
    v = np.moveaxis(np.asarray(x, np.float32).astype(ml_dtypes.bfloat16).astype(np.float64), axis, -1)
    blocks = v.reshape(v.shape[:-1] + (-1, 32))
    amax = np.abs(blocks).max(-1, keepdims=True)
    byte = np.maximum(np.where(amax > 0, np.frexp(amax)[1] - 1 + 127, 0) - down, 1)
    scale = np.exp2(byte - 127.0)
    codes = (blocks / scale).astype(np.float32).astype(dtype).astype(np.float64)
    return np.moveaxis((codes * scale).reshape(v.shape), -1, axis)


WIDE = False


def mx_kscale(k):
    if not WIDE:
        return np.ones(k)
    levels = np.array([10, -10, 5, -5, 0])
    a = np.random.permutation(np.resize(levels, k // 512 * 4)).reshape(k // 512, 4)
    idx = np.arange(k)
    return np.exp2(a[idx // 512, idx % 128 // 32])


BF16 = ml_dtypes.bfloat16


def bf(x):
    return np.asarray(x, np.float32).astype(BF16)


def f64(x):
    return np.asarray(x).astype(np.float64)


B, S, DIM, HID, R, NT = 8, 64, 1024, 2560, 128, 3
SCALING = 4.0


def lora_out(xa, bw, tw):
    return (xa @ bw) * SCALING * tw[..., None]


def setup_inputs():
    s = mx_kscale(HID)
    return {"h": bf(np.random.standard_normal((B, S, HID)) * 0.7 * s),
            "w2": bf(np.random.standard_normal((HID, DIM)) / np.sqrt(HID) / s[:, None]),
            "ha_down": bf(np.random.standard_normal((B, S, R)) * 0.7),
            "b_down": bf(np.random.standard_normal((R, DIM)) * 0.2 / np.sqrt(R)),
            "tw_down": bf(np.random.uniform(size=(B, S)))}


def reference(h, w2, ha_down, b_down, tw_down):
    base = mxq(f64(h), 2, "e4m3") @ mxq(f64(w2), 0, "e4m3")
    return base + lora_out(f64(ha_down), f64(b_down), f64(tw_down))

@@ -1,0 +1,183 @@
+from contextlib import ExitStack
+
+import concourse.mybir as mybir
+from concourse.masks import make_identity
+
+F32 = mybir.dt.float32
+BF16 = mybir.dt.bfloat16
+U32 = mybir.dt.uint32
+U8 = mybir.dt.uint8
+FP8X4 = mybir.dt.float8_e4m3fn_x4
+MULT = mybir.AluOpType.mult
+ADD = mybir.AluOpType.add
+COPY = mybir.ActivationFunctionType.Copy
+
+P = 128
+PACK = 4
+K_PASS = P * PACK
+TOKENS = 512
+K = 2560
+N = 1024
+R = 128
+SCALING = 4.0
+PASSES = K // K_PASS
+TOKEN_TILES = TOKENS // P
+BANK = 512
+HALVES = N // BANK
+PAIR_BLOCKS = 2
+PASSES_PER_BANK = BANK // (PAIR_BLOCKS * P)
+
+FLOPS = 2 * TOKENS * K * N + 2 * TOKENS * R * N
+
+
+def tile_feedforward_pb_kernel(tc, h, w2, ha_down, b_down, tw_down, out):
+    nc = tc.nc
+    h_rows = h.rearrange("b s k -> (b s) k")
+    ha_rows = ha_down.rearrange("b s r -> (b s) r")
+    out_rows = out.rearrange("b s n -> (b s) n")
+
+    with ExitStack() as ctx:
+        keep = ctx.enter_context(tc.tile_pool(name="keep", bufs=1))
+        stage = ctx.enter_context(tc.tile_pool(name="stage", bufs=3))
+        psum = ctx.enter_context(tc.psum_pool(name="psum", bufs=8))
+
+        ident_bf16 = keep.tile([P, P], BF16, name="ident_bf16")
+        make_identity(nc, ident_bf16[:])
+        ident_f32 = keep.tile([P, P], F32, name="ident_f32")
+        make_identity(nc, ident_f32[:])
+
+        tw_rows = keep.tile([P, P], BF16, name="tw_rows")
+        nc.vector.memset(tw_rows[:], 0.0)
+        nc.sync.dma_start(
+            out=tw_rows[0:TOKEN_TILES, :],
+            in_=tw_down.rearrange("(m a) s -> m (a s)", m=TOKEN_TILES),
+        )
+        ha_sb = keep.tile([P, TOKEN_TILES, R], BF16, name="ha_sb")
+        nc.sync.dma_start(out=ha_sb[:], in_=ha_rows.rearrange("(m p) r -> p m r", p=P))
+        b_sb = keep.tile([P, N], BF16, name="b_sb")
+        nc.sync.dma_start(out=b_sb[:], in_=b_down)
+
+        h_raw = []
+        for m in range(TOKEN_TILES):
+            h_raw.append(keep.tile([P, K], BF16, name="h_raw%d" % m))
+            nc.sync.dma_start(out=h_raw[m][:], in_=h_rows[m * P : (m + 1) * P, :])
+
+        w_raw = []
+        for g in range(PASSES):
+            w_raw.append(keep.tile([P, PACK, N], BF16, name="w_raw%d" % g))
+            nc.sync.dma_start(
+                out=w_raw[g][:].rearrange("q (u e) n -> q u (e n)", u=PAIR_BLOCKS),
+                in_=w2[g * K_PASS : (g + 1) * K_PASS, :].rearrange(
+                    "(u q e) n -> q u (e n)", u=PAIR_BLOCKS, q=P
+                ),
+            )
+
+        small_t = psum.tile([P, TOKEN_TILES + 1, P], BF16, name="small_t", tag="bank")
+        for m in range(TOKEN_TILES):
+            nc.tensor.transpose(small_t[:, m, :], ha_sb[:, m, :], ident_bf16[:])
+        nc.tensor.transpose(small_t[:, TOKEN_TILES, :], tw_rows[:], ident_bf16[:])
+        ha_t = keep.tile([P, TOKEN_TILES, P], BF16, name="ha_t")
+        nc.vector.tensor_copy(out=ha_t[:], in_=small_t[:, 0:TOKEN_TILES, :])
+        gain = keep.tile([P, TOKEN_TILES], F32, name="gain")
+        nc.vector.tensor_scalar(
+            out=gain[:],
+            in0=small_t[:, TOKEN_TILES, 0:TOKEN_TILES],
+            scalar1=SCALING,
+            scalar2=None,
+            op0=MULT,
+        )
+
+        h_codes = []
+        h_scales = []
+        result = []
+        for m in range(TOKEN_TILES):
+            h_words = h_raw[m][:].bitcast(F32)
+            h_grouped = keep.tile([P, PASSES * P * PACK], BF16, name="h_grouped%d" % m, align_bytes=64)
+            grouped_words = h_grouped[:].bitcast(F32).rearrange(
+                "q (g r u) -> q g r u", g=PASSES, u=PAIR_BLOCKS
+            )
+            for g0 in range(0, PASSES, PASSES_PER_BANK):
+                n_g = min(PASSES_PER_BANK, PASSES - g0)
+                h_t = psum.tile([P, n_g, PAIR_BLOCKS, P], F32, name="h_t", tag="bank")
+                for g in range(n_g):
+                    for u in range(PAIR_BLOCKS):
+                        first = ((g0 + g) * PAIR_BLOCKS + u) * P
+                        nc.tensor.transpose(
+                            h_t[:, g, u, :], h_words[:, first : first + P], ident_f32[:]
+                        )
+                nc.scalar.copy(
+                    out=grouped_words[:, g0 : g0 + n_g, :, :],
+                    in_=h_t[:].rearrange("q g u r -> q g r u"),
+                )
+
+            result.append(keep.tile([P, N], F32, name="result%d" % m))
+            for half in range(HALVES):
+                cols = slice(half * BANK, (half + 1) * BANK)
+                adapter = psum.tile([P, BANK], F32, name="adapter", tag="bank")
+                nc.tensor.matmul(
+                    out=adapter[:], lhsT=ha_t[:, m, :], rhs=b_sb[:, cols], start=True, stop=True
+                )
+                if half == 0:
+                    nc.vector.tensor_scalar(
+                        out=result[m][:, cols],
+                        in0=adapter[:],
+                        scalar1=gain[:, m : m + 1],
+                        scalar2=None,
+                        op0=MULT,
+                    )
+                else:
+                    nc.scalar.activation(
+                        out=result[m][:, cols], in_=adapter[:], func=COPY, scale=gain[:, m : m + 1]
+                    )
+
+            h_codes.append(keep.tile([P, PASSES * P], U32, name="h_codes%d" % m, align_bytes=64))
+            h_scales.append(keep.tile([P, PASSES * P], U8, name="h_scales%d" % m, align_bytes=64))
+            for first_pass, n_passes in ((0, PASSES - 1), (PASSES - 1, 1)):
+                words = slice(first_pass * P, (first_pass + n_passes) * P)
+                values = slice(first_pass * P * PACK, (first_pass + n_passes) * P * PACK)
+                nc.vector.quantize_mx(
+                    out=h_codes[m][:, words].bitcast(FP8X4),
+                    scales=h_scales[m][:, words],
+                    in_=h_grouped[:, values],
+                )
+
+        acc = [
+            [psum.tile([P, BANK], F32, name="acc%d_%d" % (m, half), tag="bank") for half in range(HALVES)]
+            for m in range(TOKEN_TILES)
+        ]
+        for g in range(PASSES):
+            w_codes = keep.tile([P, N], U32, name="w_codes%d" % g, align_bytes=64)
+            w_scales = keep.tile([P, N], U8, name="w_scales%d" % g, align_bytes=64)
+            for half in range(HALVES):
+                cols = slice(half * BANK, (half + 1) * BANK)
+                w_grouped = stage.tile([P, BANK, PACK], BF16, name="w_grouped%d" % half, align_bytes=64)
+                dst = w_grouped[:].rearrange("q (c i) t -> q c t i", i=4)
+                src = w_raw[g][:, :, cols].rearrange("q t (c i) -> q c t i", i=4)
+                if half == 0:
+                    nc.vector.tensor_copy(out=dst, in_=src)
+                else:
+                    nc.scalar.copy(out=dst, in_=src)
+                nc.vector.quantize_mx(
+                    out=w_codes[:, cols].bitcast(FP8X4),
+                    scales=w_scales[:, cols],
+                    in_=w_grouped[:].rearrange("q n t -> q (n t)"),
+                )
+                this_pass = slice(g * P, (g + 1) * P)
+                for m in range(TOKEN_TILES):
+                    nc.tensor.matmul_mx(
+                        out=acc[m][half][:],
+                        lhsT=h_codes[m][:, this_pass].bitcast(FP8X4),
+                        lhsT_scale=h_scales[m][:, this_pass],
+                        rhs=w_codes[:, cols].bitcast(FP8X4),
+                        rhs_scale=w_scales[:, cols],
+                        start=(g == 0),
+                        stop=(g == PASSES - 1),
+                    )
+
+        for half in range(HALVES):
+            cols = slice(half * BANK, (half + 1) * BANK)
+            for m in range(TOKEN_TILES):
+                nc.vector.tensor_tensor(
+                    out=result[m][:, cols], in0=acc[m][half][:], in1=result[m][:, cols], op=ADD
+                )
+                nc.sync.dma_start(out=out_rows[m * P : (m + 1) * P, cols], in_=result[m][:, cols])

@@ -24,6 +24,8 @@ PASSES = K // K_PASS
 TOKEN_TILES = TOKENS // P
 BANK = 512
 HALVES = N // BANK
+LEFT = 0
+RIGHT = 1
 PAIR_BLOCKS = 2
 PASSES_PER_BANK = BANK // (PAIR_BLOCKS * P)
 
@@ -37,8 +39,8 @@ def tile_feedforward_pb_kernel(tc, h, w2, ha_down, b_down, tw_down, out):
     out_rows = out.rearrange("b s n -> (b s) n")
 
     with ExitStack() as ctx:
+        ctx.enter_context(tc.manual_schedule())
         keep = ctx.enter_context(tc.tile_pool(name="keep", bufs=1))
-        stage = ctx.enter_context(tc.tile_pool(name="stage", bufs=3))
         psum = ctx.enter_context(tc.psum_pool(name="psum", bufs=8))
 
         ident_bf16 = keep.tile([P, P], BF16, name="ident_bf16")
@@ -57,20 +59,22 @@ def tile_feedforward_pb_kernel(tc, h, w2, ha_down, b_down, tw_down, out):
         b_sb = keep.tile([P, N], BF16, name="b_sb")
         nc.sync.dma_start(out=b_sb[:], in_=b_down)
 
-        h_raw = []
-        for m in range(TOKEN_TILES):
-            h_raw.append(keep.tile([P, K], BF16, name="h_raw%d" % m))
-            nc.sync.dma_start(out=h_raw[m][:], in_=h_rows[m * P : (m + 1) * P, :])
+        w_raw = [keep.tile([P, PACK, N], BF16, name="w_raw%d" % g) for g in range(PASSES)]
+        h_raw = [keep.tile([P, K], BF16, name="h_raw%d" % m) for m in range(TOKEN_TILES)]
 
-        w_raw = []
-        for g in range(PASSES):
-            w_raw.append(keep.tile([P, PACK, N], BF16, name="w_raw%d" % g))
+        def load_w(g):
             nc.sync.dma_start(
                 out=w_raw[g][:].rearrange("q (u e) n -> q u (e n)", u=PAIR_BLOCKS),
                 in_=w2[g * K_PASS : (g + 1) * K_PASS, :].rearrange(
                     "(u q e) n -> q u (e n)", u=PAIR_BLOCKS, q=P
                 ),
             )
+
+        load_w(0)
+        for m in range(TOKEN_TILES):
+            nc.sync.dma_start(out=h_raw[m][:], in_=h_rows[m * P : (m + 1) * P, :])
+        for g in range(1, PASSES):
+            load_w(g)
 
         small_t = psum.tile([P, TOKEN_TILES + 1, P], BF16, name="small_t", tag="bank")
         for m in range(TOKEN_TILES):
@@ -86,10 +90,71 @@ def tile_feedforward_pb_kernel(tc, h, w2, ha_down, b_down, tw_down, out):
             scalar2=None,
             op0=MULT,
         )
+        result = [keep.tile([P, N], F32, name="result%d" % m) for m in range(TOKEN_TILES)]
 
-        h_codes = []
-        h_scales = []
-        result = []
+        def adapter_product(m, half):
+            cols = slice(half * BANK, (half + 1) * BANK)
+            adapter = psum.tile([P, BANK], F32, name="adapter", tag="bank")
+            nc.tensor.matmul(
+                out=adapter[:], lhsT=ha_t[:, m, :], rhs=b_sb[:, cols], start=True, stop=True
+            )
+            return adapter
+
+        for m in range(TOKEN_TILES):
+            adapter = adapter_product(m, LEFT)
+            nc.vector.tensor_scalar(
+                out=result[m][:, 0:BANK],
+                in0=adapter[:],
+                scalar1=gain[:, m : m + 1],
+                scalar2=None,
+                op0=MULT,
+            )
+
+        w_grouped = [
+            [keep.tile([P, BANK, PACK], BF16, name="w_grouped%d_%d" % (g, half), align_bytes=64) for half in range(HALVES)]
+            for g in range(PASSES)
+        ]
+        w_codes = [keep.tile([P, N], U32, name="w_codes%d" % g, align_bytes=64) for g in range(PASSES)]
+        w_scales = [keep.tile([P, N], U8, name="w_scales%d" % g, align_bytes=64) for g in range(PASSES)]
+        h_codes = [keep.tile([P, PASSES * P], U32, name="h_codes%d" % m, align_bytes=64) for m in range(TOKEN_TILES)]
+        h_scales = [keep.tile([P, PASSES * P], U8, name="h_scales%d" % m, align_bytes=64) for m in range(TOKEN_TILES)]
+        acc = []
+
+        def regroup(g, half):
+            cols = slice(half * BANK, (half + 1) * BANK)
+            dst = w_grouped[g][half][:].rearrange("q (c i) t -> q c t i", i=4)
+            src = w_raw[g][:, :, cols].rearrange("q t (c i) -> q c t i", i=4)
+            if half == LEFT:
+                nc.vector.tensor_copy(out=dst, in_=src)
+            else:
+                nc.scalar.copy(out=dst, in_=src)
+
+        def quantise(g, half):
+            cols = slice(half * BANK, (half + 1) * BANK)
+            nc.vector.quantize_mx(
+                out=w_codes[g][:, cols].bitcast(FP8X4),
+                scales=w_scales[g][:, cols],
+                in_=w_grouped[g][half][:].rearrange("q n t -> q (n t)"),
+            )
+
+        def multiply(g, half):
+            cols = slice(half * BANK, (half + 1) * BANK)
+            this_pass = slice(g * P, (g + 1) * P)
+            for m in range(TOKEN_TILES):
+                nc.tensor.matmul_mx(
+                    out=acc[m][half][:],
+                    lhsT=h_codes[m][:, this_pass].bitcast(FP8X4),
+                    lhsT_scale=h_scales[m][:, this_pass],
+                    rhs=w_codes[g][:, cols].bitcast(FP8X4),
+                    rhs_scale=w_scales[g][:, cols],
+                    start=(g == 0),
+                    stop=(g == PASSES - 1),
+                )
+
+        regroup(0, RIGHT)
+        regroup(0, LEFT)
+        quantise(0, LEFT)
+
         for m in range(TOKEN_TILES):
             h_words = h_raw[m][:].bitcast(F32)
             h_grouped = keep.tile([P, PASSES * P * PACK], BF16, name="h_grouped%d" % m, align_bytes=64)
@@ -109,29 +174,6 @@ def tile_feedforward_pb_kernel(tc, h, w2, ha_down, b_down, tw_down, out):
                     out=grouped_words[:, g0 : g0 + n_g, :, :],
                     in_=h_t[:].rearrange("q g u r -> q g r u"),
                 )
-
-            result.append(keep.tile([P, N], F32, name="result%d" % m))
-            for half in range(HALVES):
-                cols = slice(half * BANK, (half + 1) * BANK)
-                adapter = psum.tile([P, BANK], F32, name="adapter", tag="bank")
-                nc.tensor.matmul(
-                    out=adapter[:], lhsT=ha_t[:, m, :], rhs=b_sb[:, cols], start=True, stop=True
-                )
-                if half == 0:
-                    nc.vector.tensor_scalar(
-                        out=result[m][:, cols],
-                        in0=adapter[:],
-                        scalar1=gain[:, m : m + 1],
-                        scalar2=None,
-                        op0=MULT,
-                    )
-                else:
-                    nc.scalar.activation(
-                        out=result[m][:, cols], in_=adapter[:], func=COPY, scale=gain[:, m : m + 1]
-                    )
-
-            h_codes.append(keep.tile([P, PASSES * P], U32, name="h_codes%d" % m, align_bytes=64))
-            h_scales.append(keep.tile([P, PASSES * P], U8, name="h_scales%d" % m, align_bytes=64))
             for first_pass, n_passes in ((0, PASSES - 1), (PASSES - 1, 1)):
                 words = slice(first_pass * P, (first_pass + n_passes) * P)
                 values = slice(first_pass * P * PACK, (first_pass + n_passes) * P * PACK)
@@ -141,43 +183,33 @@ def tile_feedforward_pb_kernel(tc, h, w2, ha_down, b_down, tw_down, out):
                     in_=h_grouped[:, values],
                 )
 
-        acc = [
-            [psum.tile([P, BANK], F32, name="acc%d_%d" % (m, half), tag="bank") for half in range(HALVES)]
-            for m in range(TOKEN_TILES)
-        ]
-        for g in range(PASSES):
-            w_codes = keep.tile([P, N], U32, name="w_codes%d" % g, align_bytes=64)
-            w_scales = keep.tile([P, N], U8, name="w_scales%d" % g, align_bytes=64)
-            for half in range(HALVES):
-                cols = slice(half * BANK, (half + 1) * BANK)
-                w_grouped = stage.tile([P, BANK, PACK], BF16, name="w_grouped%d" % half, align_bytes=64)
-                dst = w_grouped[:].rearrange("q (c i) t -> q c t i", i=4)
-                src = w_raw[g][:, :, cols].rearrange("q t (c i) -> q c t i", i=4)
-                if half == 0:
-                    nc.vector.tensor_copy(out=dst, in_=src)
-                else:
-                    nc.scalar.copy(out=dst, in_=src)
-                nc.vector.quantize_mx(
-                    out=w_codes[:, cols].bitcast(FP8X4),
-                    scales=w_scales[:, cols],
-                    in_=w_grouped[:].rearrange("q n t -> q (n t)"),
-                )
-                this_pass = slice(g * P, (g + 1) * P)
-                for m in range(TOKEN_TILES):
-                    nc.tensor.matmul_mx(
-                        out=acc[m][half][:],
-                        lhsT=h_codes[m][:, this_pass].bitcast(FP8X4),
-                        lhsT_scale=h_scales[m][:, this_pass],
-                        rhs=w_codes[:, cols].bitcast(FP8X4),
-                        rhs_scale=w_scales[:, cols],
-                        start=(g == 0),
-                        stop=(g == PASSES - 1),
-                    )
+        for m in range(TOKEN_TILES):
+            acc.append([psum.tile([P, BANK], F32, name="acc%d_%d" % (m, half), tag="bank") for half in range(HALVES)])
+        multiply(0, LEFT)
+        for g in range(1, PASSES):
+            regroup(g, RIGHT)
+            quantise(g - 1, RIGHT)
+            multiply(g - 1, RIGHT)
+            regroup(g, LEFT)
+            quantise(g, LEFT)
+            multiply(g, LEFT)
+        quantise(PASSES - 1, RIGHT)
+        multiply(PASSES - 1, RIGHT)
 
-        for half in range(HALVES):
-            cols = slice(half * BANK, (half + 1) * BANK)
-            for m in range(TOKEN_TILES):
-                nc.vector.tensor_tensor(
-                    out=result[m][:, cols], in0=acc[m][half][:], in1=result[m][:, cols], op=ADD
-                )
-                nc.sync.dma_start(out=out_rows[m * P : (m + 1) * P, cols], in_=result[m][:, cols])
+        for m in range(TOKEN_TILES):
+            nc.vector.tensor_tensor(
+                out=result[m][:, 0:BANK], in0=acc[m][LEFT][:], in1=result[m][:, 0:BANK], op=ADD
+            )
+            nc.sync.dma_start(out=out_rows[m * P : (m + 1) * P, 0:BANK], in_=result[m][:, 0:BANK])
+        for m in range(TOKEN_TILES):
+            nc.scalar.copy(out=result[m][:, BANK:N], in_=acc[m][RIGHT][:])
+            adapter = adapter_product(m, RIGHT)
+            nc.vector.scalar_tensor_tensor(
+                out=result[m][:, BANK:N],
+                in0=adapter[:],
+                scalar=gain[:, m : m + 1],
+                in1=result[m][:, BANK:N],
+                op0=MULT,
+                op1=ADD,
+            )
+            nc.sync.dma_start(out=out_rows[m * P : (m + 1) * P, BANK:N], in_=result[m][:, BANK:N])

@@ -48,16 +48,16 @@ def tile_feedforward_pb_kernel(tc, h, w2, ha_down, b_down, tw_down, out):
         ident_f32 = keep.tile([P, P], F32, name="ident_f32")
         make_identity(nc, ident_f32[:])
 
+        ha_sb = keep.tile([P, TOKEN_TILES, R], BF16, name="ha_sb")
+        nc.sync.dma_start(out=ha_sb[:], in_=ha_rows.rearrange("(m p) r -> p m r", p=P))
+        b_sb = keep.tile([P, N], BF16, name="b_sb")
+        nc.sync.dma_start(out=b_sb[:], in_=b_down)
         tw_rows = keep.tile([P, P], BF16, name="tw_rows")
         nc.vector.memset(tw_rows[:], 0.0)
         nc.sync.dma_start(
             out=tw_rows[0:TOKEN_TILES, :],
             in_=tw_down.rearrange("(m a) s -> m (a s)", m=TOKEN_TILES),
         )
-        ha_sb = keep.tile([P, TOKEN_TILES, R], BF16, name="ha_sb")
-        nc.sync.dma_start(out=ha_sb[:], in_=ha_rows.rearrange("(m p) r -> p m r", p=P))
-        b_sb = keep.tile([P, N], BF16, name="b_sb")
-        nc.sync.dma_start(out=b_sb[:], in_=b_down)
 
         w_raw = [keep.tile([P, PACK, N], BF16, name="w_raw%d" % g) for g in range(PASSES)]
         h_raw = [keep.tile([P, K], BF16, name="h_raw%d" % m) for m in range(TOKEN_TILES)]
@@ -154,6 +154,7 @@ def tile_feedforward_pb_kernel(tc, h, w2, ha_down, b_down, tw_down, out):
         regroup(0, RIGHT)
         regroup(0, LEFT)
         quantise(0, LEFT)
+        quantise(0, RIGHT)
 
         for m in range(TOKEN_TILES):
             h_words = h_raw[m][:].bitcast(F32)
@@ -186,10 +187,12 @@ def tile_feedforward_pb_kernel(tc, h, w2, ha_down, b_down, tw_down, out):
         for m in range(TOKEN_TILES):
             acc.append([psum.tile([P, BANK], F32, name="acc%d_%d" % (m, half), tag="bank") for half in range(HALVES)])
         multiply(0, LEFT)
+        multiply(0, RIGHT)
         for g in range(1, PASSES):
             regroup(g, RIGHT)
-            quantise(g - 1, RIGHT)
-            multiply(g - 1, RIGHT)
+            if g > 1:
+                quantise(g - 1, RIGHT)
+                multiply(g - 1, RIGHT)
             regroup(g, LEFT)
             quantise(g, LEFT)
             multiply(g, LEFT)

@@ -64,10 +64,8 @@ def tile_feedforward_pb_kernel(tc, h, w2, ha_down, b_down, tw_down, out):
 
         def load_w(g):
             nc.sync.dma_start(
-                out=w_raw[g][:].rearrange("q (u e) n -> q u (e n)", u=PAIR_BLOCKS),
-                in_=w2[g * K_PASS : (g + 1) * K_PASS, :].rearrange(
-                    "(u q e) n -> q u (e n)", u=PAIR_BLOCKS, q=P
-                ),
+                out=w_raw[g][:],
+                in_=w2[g * K_PASS : (g + 1) * K_PASS, :].rearrange("(q t) n -> q t n", t=PACK),
             )
 
         load_w(0)
@@ -167,9 +165,11 @@ def tile_feedforward_pb_kernel(tc, h, w2, ha_down, b_down, tw_down, out):
                 h_t = psum.tile([P, n_g, PAIR_BLOCKS, P], F32, name="h_t", tag="bank")
                 for g in range(n_g):
                     for u in range(PAIR_BLOCKS):
-                        first = ((g0 + g) * PAIR_BLOCKS + u) * P
+                        first = (g0 + g) * PAIR_BLOCKS * P + u
                         nc.tensor.transpose(
-                            h_t[:, g, u, :], h_words[:, first : first + P], ident_f32[:]
+                            h_t[:, g, u, :],
+                            h_words[:, first : first + PAIR_BLOCKS * P - u : PAIR_BLOCKS],
+                            ident_f32[:],
                         )
                 nc.scalar.copy(
                     out=grouped_words[:, g0 : g0 + n_g, :, :],

@@ -10,7 +10,6 @@ U8 = mybir.dt.uint8
 FP8X4 = mybir.dt.float8_e4m3fn_x4
 MULT = mybir.AluOpType.mult
 ADD = mybir.AluOpType.add
-COPY = mybir.ActivationFunctionType.Copy
 
 P = 128
 PACK = 4
@@ -21,27 +20,32 @@ N = 1024
 R = 128
 SCALING = 4.0
 PASSES = K // K_PASS
+LAST = PASSES - 1
 TOKEN_TILES = TOKENS // P
 BANK = 512
 HALVES = N // BANK
 LEFT = 0
 RIGHT = 1
-PAIR_BLOCKS = 2
-PASSES_PER_BANK = BANK // (PAIR_BLOCKS * P)
+PAIRS = 2
+PER_BANK = BANK // (PAIRS * P)
 
 FLOPS = 2 * TOKENS * K * N + 2 * TOKENS * R * N
 
 
 def tile_feedforward_pb_kernel(tc, h, w2, ha_down, b_down, tw_down, out):
     nc = tc.nc
-    h_rows = h.rearrange("b s k -> (b s) k")
-    ha_rows = ha_down.rearrange("b s r -> (b s) r")
-    out_rows = out.rearrange("b s n -> (b s) n")
+    h_rows = h.rearrange("b s k -> (b s) k").rearrange("(p m) k -> p m k", m=TOKEN_TILES)
+    ha_rows = ha_down.rearrange("b s r -> (b s) r").rearrange("(p m) r -> p m r", m=TOKEN_TILES)
+    tw_rows = tw_down.rearrange("b s -> (b s)").rearrange("(p m) -> p m", m=TOKEN_TILES)
+    out_rows = out.rearrange("b s n -> (b s) n").rearrange("(p m) n -> p m n", m=TOKEN_TILES)
 
     with ExitStack() as ctx:
         ctx.enter_context(tc.manual_schedule())
         keep = ctx.enter_context(tc.tile_pool(name="keep", bufs=1))
         psum = ctx.enter_context(tc.psum_pool(name="psum", bufs=8))
+
+        def half_cols(half):
+            return slice(half * BANK, (half + 1) * BANK)
 
         ident_bf16 = keep.tile([P, P], BF16, name="ident_bf16")
         make_identity(nc, ident_bf16[:])
@@ -49,15 +53,11 @@ def tile_feedforward_pb_kernel(tc, h, w2, ha_down, b_down, tw_down, out):
         make_identity(nc, ident_f32[:])
 
         ha_sb = keep.tile([P, TOKEN_TILES, R], BF16, name="ha_sb")
-        nc.sync.dma_start(out=ha_sb[:], in_=ha_rows.rearrange("(m p) r -> p m r", p=P))
+        nc.sync.dma_start(out=ha_sb[:], in_=ha_rows)
         b_sb = keep.tile([P, N], BF16, name="b_sb")
         nc.sync.dma_start(out=b_sb[:], in_=b_down)
-        tw_rows = keep.tile([P, P], BF16, name="tw_rows")
-        nc.vector.memset(tw_rows[:], 0.0)
-        nc.sync.dma_start(
-            out=tw_rows[0:TOKEN_TILES, :],
-            in_=tw_down.rearrange("(m a) s -> m (a s)", m=TOKEN_TILES),
-        )
+        tw_sb = keep.tile([P, TOKEN_TILES], BF16, name="tw_sb")
+        nc.sync.dma_start(out=tw_sb[:], in_=tw_rows)
 
         w_raw = [keep.tile([P, PACK, N], BF16, name="w_raw%d" % g) for g in range(PASSES)]
         h_raw = [keep.tile([P, K], BF16, name="h_raw%d" % m) for m in range(TOKEN_TILES)]
@@ -68,44 +68,62 @@ def tile_feedforward_pb_kernel(tc, h, w2, ha_down, b_down, tw_down, out):
                 in_=w2[g * K_PASS : (g + 1) * K_PASS, :].rearrange("(q t) n -> q t n", t=PACK),
             )
 
+        def load_h(m):
+            nc.sync.dma_start(out=h_raw[m][:], in_=h_rows[:, m, :])
+
         load_w(0)
-        for m in range(TOKEN_TILES):
-            nc.sync.dma_start(out=h_raw[m][:], in_=h_rows[m * P : (m + 1) * P, :])
-        for g in range(1, PASSES):
+        load_h(0)
+        load_h(1)
+        load_w(1)
+        load_h(2)
+        load_h(3)
+        for g in range(2, PASSES):
             load_w(g)
 
-        small_t = psum.tile([P, TOKEN_TILES + 1, P], BF16, name="small_t", tag="bank")
-        for m in range(TOKEN_TILES):
-            nc.tensor.transpose(small_t[:, m, :], ha_sb[:, m, :], ident_bf16[:])
-        nc.tensor.transpose(small_t[:, TOKEN_TILES, :], tw_rows[:], ident_bf16[:])
-        ha_t = keep.tile([P, TOKEN_TILES, P], BF16, name="ha_t")
-        nc.vector.tensor_copy(out=ha_t[:], in_=small_t[:, 0:TOKEN_TILES, :])
-        gain = keep.tile([P, TOKEN_TILES], F32, name="gain")
-        nc.vector.tensor_scalar(
-            out=gain[:],
-            in0=small_t[:, TOKEN_TILES, 0:TOKEN_TILES],
-            scalar1=SCALING,
-            scalar2=None,
-            op0=MULT,
-        )
-        result = [keep.tile([P, N], F32, name="result%d" % m) for m in range(TOKEN_TILES)]
+        h_grouped = [keep.tile([P, LAST, P, PACK], BF16, name="h_grouped%d" % m, align_bytes=64) for m in range(TOKEN_TILES)]
+        h_codes = [keep.tile([P, LAST * P], U32, name="h_codes%d" % m, align_bytes=64) for m in range(TOKEN_TILES)]
+        h_scales = [keep.tile([P, LAST * P], U8, name="h_scales%d" % m, align_bytes=64) for m in range(TOKEN_TILES)]
+        last_grouped = keep.tile([P, TOKEN_TILES, P, PACK], BF16, name="last_grouped", align_bytes=64)
+        last_codes = keep.tile([P, TOKEN_TILES * P], U32, name="last_codes", align_bytes=64)
+        last_scales = keep.tile([P, TOKEN_TILES * P], U8, name="last_scales", align_bytes=64)
 
-        def adapter_product(m, half):
-            cols = slice(half * BANK, (half + 1) * BANK)
-            adapter = psum.tile([P, BANK], F32, name="adapter", tag="bank")
-            nc.tensor.matmul(
-                out=adapter[:], lhsT=ha_t[:, m, :], rhs=b_sb[:, cols], start=True, stop=True
+        def transpose_bank(blocks):
+            bank = psum.tile([P, PER_BANK, PAIRS, P], F32, name="h_t", tag="bank")
+            for i, (m, g) in enumerate(blocks):
+                words = h_raw[m][:].bitcast(F32)
+                for u in range(PAIRS):
+                    first = g * PAIRS * P + u
+                    nc.tensor.transpose(
+                        bank[:, i, u, :], words[:, first : first + PAIRS * P - u : PAIRS], ident_f32[:]
+                    )
+            return bank
+
+        def group_bank(copy, bank, grouped):
+            copy(
+                out=grouped.rearrange("q i r t -> q i (r t)").bitcast(F32).rearrange("q i (r u) -> q i r u", u=PAIRS),
+                in_=bank[:].rearrange("q i u r -> q i r u"),
             )
-            return adapter
 
-        for m in range(TOKEN_TILES):
-            adapter = adapter_product(m, LEFT)
-            nc.vector.tensor_scalar(
-                out=result[m][:, 0:BANK],
-                in0=adapter[:],
-                scalar1=gain[:, m : m + 1],
-                scalar2=None,
-                op0=MULT,
+        def transpose_tile(m):
+            return [transpose_bank([(m, g0 + i) for i in range(PER_BANK)]) for g0 in range(0, LAST, PER_BANK)]
+
+        def group_tile(m, banks):
+            for i, bank in enumerate(banks):
+                group_bank(nc.scalar.copy, bank, h_grouped[m][:, i * PER_BANK : (i + 1) * PER_BANK, :, :])
+
+        def quantise_tile(m):
+            nc.vector.quantize_mx(
+                out=h_codes[m][:].bitcast(FP8X4),
+                scales=h_scales[m][:],
+                in_=h_grouped[m][:].rearrange("q g r t -> q (g r t)"),
+            )
+
+        def quantise_last(m0):
+            words = slice(m0 * P, (m0 + PER_BANK) * P)
+            nc.vector.quantize_mx(
+                out=last_codes[:, words].bitcast(FP8X4),
+                scales=last_scales[:, words],
+                in_=last_grouped[:, m0 : m0 + PER_BANK, :, :].rearrange("q m r t -> q (m r t)"),
             )
 
         w_grouped = [
@@ -114,105 +132,128 @@ def tile_feedforward_pb_kernel(tc, h, w2, ha_down, b_down, tw_down, out):
         ]
         w_codes = [keep.tile([P, N], U32, name="w_codes%d" % g, align_bytes=64) for g in range(PASSES)]
         w_scales = [keep.tile([P, N], U8, name="w_scales%d" % g, align_bytes=64) for g in range(PASSES)]
-        h_codes = [keep.tile([P, PASSES * P], U32, name="h_codes%d" % m, align_bytes=64) for m in range(TOKEN_TILES)]
-        h_scales = [keep.tile([P, PASSES * P], U8, name="h_scales%d" % m, align_bytes=64) for m in range(TOKEN_TILES)]
-        acc = []
 
         def regroup(g, half):
-            cols = slice(half * BANK, (half + 1) * BANK)
             dst = w_grouped[g][half][:].rearrange("q (c i) t -> q c t i", i=4)
-            src = w_raw[g][:, :, cols].rearrange("q t (c i) -> q c t i", i=4)
+            src = w_raw[g][:, :, half_cols(half)].rearrange("q t (c i) -> q c t i", i=4)
             if half == LEFT:
                 nc.vector.tensor_copy(out=dst, in_=src)
             else:
                 nc.scalar.copy(out=dst, in_=src)
 
         def quantise(g, half):
-            cols = slice(half * BANK, (half + 1) * BANK)
             nc.vector.quantize_mx(
-                out=w_codes[g][:, cols].bitcast(FP8X4),
-                scales=w_scales[g][:, cols],
+                out=w_codes[g][:, half_cols(half)].bitcast(FP8X4),
+                scales=w_scales[g][:, half_cols(half)],
                 in_=w_grouped[g][half][:].rearrange("q n t -> q (n t)"),
             )
 
-        def multiply(g, half):
-            cols = slice(half * BANK, (half + 1) * BANK)
-            this_pass = slice(g * P, (g + 1) * P)
-            for m in range(TOKEN_TILES):
-                nc.tensor.matmul_mx(
-                    out=acc[m][half][:],
-                    lhsT=h_codes[m][:, this_pass].bitcast(FP8X4),
-                    lhsT_scale=h_scales[m][:, this_pass],
-                    rhs=w_codes[g][:, cols].bitcast(FP8X4),
-                    rhs_scale=w_scales[g][:, cols],
-                    start=(g == 0),
-                    stop=(g == PASSES - 1),
-                )
+        acc = {}
+
+        def multiply(g, m, half):
+            if g == 0:
+                acc[m, half] = psum.tile([P, BANK], F32, name="acc%d_%d" % (m, half), tag="bank")
+            if g == LAST:
+                h_words, planes, words = last_codes, last_scales, slice(m * P, (m + 1) * P)
+            else:
+                h_words, planes, words = h_codes[m], h_scales[m], slice(g * P, (g + 1) * P)
+            nc.tensor.matmul_mx(
+                out=acc[m, half][:],
+                lhsT=h_words[:, words].bitcast(FP8X4),
+                lhsT_scale=planes[:, words],
+                rhs=w_codes[g][:, half_cols(half)].bitcast(FP8X4),
+                rhs_scale=w_scales[g][:, half_cols(half)],
+                start=(g == 0),
+                stop=(g == LAST),
+            )
+
+        result = [keep.tile([P, N], F32, name="result%d" % m) for m in range(TOKEN_TILES)]
+        ha_t = keep.tile([P, TOKEN_TILES, P], BF16, name="ha_t")
+        gain = keep.tile([P, TOKEN_TILES], F32, name="gain")
+
+        def adapter_product(m, half):
+            bank = psum.tile([P, BANK], F32, name="adapter", tag="bank")
+            nc.tensor.matmul(
+                out=bank[:], lhsT=ha_t[:, m, :], rhs=b_sb[:, half_cols(half)], start=True, stop=True
+            )
+            return bank
+
+        ha_bank = psum.tile([P, TOKEN_TILES, P], BF16, name="ha_bank", tag="bank")
+        for m in range(TOKEN_TILES):
+            nc.tensor.transpose(ha_bank[:, m, :], ha_sb[:, m, :], ident_bf16[:])
+        nc.vector.tensor_copy(out=ha_t[:], in_=ha_bank[:])
+        nc.vector.tensor_scalar(out=gain[:], in0=tw_sb[:], scalar1=SCALING, scalar2=None, op0=MULT)
+
+        for m in range(TOKEN_TILES):
+            bank = adapter_product(m, LEFT)
+            nc.vector.tensor_scalar(
+                out=result[m][:, half_cols(LEFT)], in0=bank[:], scalar1=gain[:, m : m + 1], scalar2=None, op0=MULT
+            )
 
         regroup(0, RIGHT)
         regroup(0, LEFT)
         quantise(0, LEFT)
         quantise(0, RIGHT)
 
-        for m in range(TOKEN_TILES):
-            h_words = h_raw[m][:].bitcast(F32)
-            h_grouped = keep.tile([P, PASSES * P * PACK], BF16, name="h_grouped%d" % m, align_bytes=64)
-            grouped_words = h_grouped[:].bitcast(F32).rearrange(
-                "q (g r u) -> q g r u", g=PASSES, u=PAIR_BLOCKS
-            )
-            for g0 in range(0, PASSES, PASSES_PER_BANK):
-                n_g = min(PASSES_PER_BANK, PASSES - g0)
-                h_t = psum.tile([P, n_g, PAIR_BLOCKS, P], F32, name="h_t", tag="bank")
-                for g in range(n_g):
-                    for u in range(PAIR_BLOCKS):
-                        first = (g0 + g) * PAIR_BLOCKS * P + u
-                        nc.tensor.transpose(
-                            h_t[:, g, u, :],
-                            h_words[:, first : first + PAIR_BLOCKS * P - u : PAIR_BLOCKS],
-                            ident_f32[:],
-                        )
-                nc.scalar.copy(
-                    out=grouped_words[:, g0 : g0 + n_g, :, :],
-                    in_=h_t[:].rearrange("q g u r -> q g r u"),
-                )
-            for first_pass, n_passes in ((0, PASSES - 1), (PASSES - 1, 1)):
-                words = slice(first_pass * P, (first_pass + n_passes) * P)
-                values = slice(first_pass * P * PACK, (first_pass + n_passes) * P * PACK)
-                nc.vector.quantize_mx(
-                    out=h_codes[m][:, words].bitcast(FP8X4),
-                    scales=h_scales[m][:, words],
-                    in_=h_grouped[:, values],
-                )
+        tile0 = transpose_tile(0)
+        tile1 = transpose_tile(1)
+        group_tile(0, tile0)
+        last01 = transpose_bank([(0, LAST), (1, LAST)])
+        quantise_tile(0)
+        group_tile(1, tile1)
+        group_bank(nc.vector.tensor_copy, last01, last_grouped[:, 0:PER_BANK, :, :])
+        quantise_tile(1)
+        for m in (0, 1):
+            for half in range(HALVES):
+                multiply(0, m, half)
+        regroup(1, RIGHT)
+        regroup(1, LEFT)
+        quantise_last(0)
+        quantise(1, LEFT)
+        quantise(1, RIGHT)
 
-        for m in range(TOKEN_TILES):
-            acc.append([psum.tile([P, BANK], F32, name="acc%d_%d" % (m, half), tag="bank") for half in range(HALVES)])
-        multiply(0, LEFT)
-        multiply(0, RIGHT)
-        for g in range(1, PASSES):
-            regroup(g, RIGHT)
-            if g > 1:
-                quantise(g - 1, RIGHT)
-                multiply(g - 1, RIGHT)
-            regroup(g, LEFT)
-            quantise(g, LEFT)
-            multiply(g, LEFT)
-        quantise(PASSES - 1, RIGHT)
-        multiply(PASSES - 1, RIGHT)
+        tile2 = transpose_tile(2)
+        tile3 = transpose_tile(3)
+        group_tile(2, tile2)
+        last23 = transpose_bank([(2, LAST), (3, LAST)])
+        quantise_tile(2)
+        group_tile(3, tile3)
+        group_bank(nc.vector.tensor_copy, last23, last_grouped[:, PER_BANK:, :, :])
+        for m in (0, 1):
+            for half in range(HALVES):
+                multiply(1, m, half)
+
+        regroup(2, RIGHT)
+        regroup(2, LEFT)
+        quantise_tile(3)
+        quantise_last(2)
+        for m in (2, 3):
+            for g in (0, 1):
+                for half in range(HALVES):
+                    multiply(g, m, half)
+        for g in range(2, PASSES):
+            if g > 2:
+                regroup(g, RIGHT)
+                regroup(g, LEFT)
+            for half in range(HALVES):
+                quantise(g, half)
+                for m in range(TOKEN_TILES):
+                    multiply(g, m, half)
 
         for m in range(TOKEN_TILES):
             nc.vector.tensor_tensor(
-                out=result[m][:, 0:BANK], in0=acc[m][LEFT][:], in1=result[m][:, 0:BANK], op=ADD
+                out=result[m][:, half_cols(LEFT)], in0=acc[m, LEFT][:], in1=result[m][:, half_cols(LEFT)], op=ADD
             )
-            nc.sync.dma_start(out=out_rows[m * P : (m + 1) * P, 0:BANK], in_=result[m][:, 0:BANK])
+            nc.sync.dma_start(out=out_rows[:, m, half_cols(LEFT)], in_=result[m][:, half_cols(LEFT)])
         for m in range(TOKEN_TILES):
-            nc.scalar.copy(out=result[m][:, BANK:N], in_=acc[m][RIGHT][:])
-            adapter = adapter_product(m, RIGHT)
+            nc.scalar.copy(out=result[m][:, half_cols(RIGHT)], in_=acc[m, RIGHT][:])
+            bank = adapter_product(m, RIGHT)
             nc.vector.scalar_tensor_tensor(
-                out=result[m][:, BANK:N],
-                in0=adapter[:],
+                out=result[m][:, half_cols(RIGHT)],
+                in0=bank[:],
                 scalar=gain[:, m : m + 1],
-                in1=result[m][:, BANK:N],
+                in1=result[m][:, half_cols(RIGHT)],
                 op0=MULT,
                 op1=ADD,
             )
-            nc.sync.dma_start(out=out_rows[m * P : (m + 1) * P, BANK:N], in_=result[m][:, BANK:N])
+            nc.sync.dma_start(out=out_rows[:, m, half_cols(RIGHT)], in_=result[m][:, half_cols(RIGHT)])

@@ -10,6 +10,7 @@ U8 = mybir.dt.uint8
 FP8X4 = mybir.dt.float8_e4m3fn_x4
 MULT = mybir.AluOpType.mult
 ADD = mybir.AluOpType.add
+COPY = mybir.ActivationFunctionType.Copy
 
 P = 128
 PACK = 4
@@ -26,7 +27,10 @@ BANK = 512
 HALVES = N // BANK
 LEFT = 0
 RIGHT = 1
+WHOLE = 2
+SPLIT = 3
 PAIRS = 2
+VECTOR_FROM = 896
 PER_BANK = BANK // (PAIRS * P)
 
 FLOPS = 2 * TOKENS * K * N + 2 * TOKENS * R * N
@@ -59,26 +63,32 @@ def tile_feedforward_pb_kernel(tc, h, w2, ha_down, b_down, tw_down, out):
         tw_sb = keep.tile([P, TOKEN_TILES], BF16, name="tw_sb")
         nc.sync.dma_start(out=tw_sb[:], in_=tw_rows)
 
-        w_raw = [keep.tile([P, PACK, N], BF16, name="w_raw%d" % g) for g in range(PASSES)]
+        w_raw = {}
+        for g in range(PASSES):
+            for half in range(HALVES) if g >= SPLIT else [WHOLE]:
+                w_raw[g, half] = keep.tile([P, PACK, N if half == WHOLE else BANK], BF16, name="w_raw%d_%d" % (g, half))
         h_raw = [keep.tile([P, K], BF16, name="h_raw%d" % m) for m in range(TOKEN_TILES)]
 
-        def load_w(g):
+        def load_w(g, half):
+            cols = slice(0, N) if half == WHOLE else half_cols(half)
             nc.sync.dma_start(
-                out=w_raw[g][:],
-                in_=w2[g * K_PASS : (g + 1) * K_PASS, :].rearrange("(q t) n -> q t n", t=PACK),
+                out=w_raw[g, half][:],
+                in_=w2[g * K_PASS : (g + 1) * K_PASS, cols].rearrange("(q t) n -> q t n", t=PACK),
             )
 
         def load_h(m):
             nc.sync.dma_start(out=h_raw[m][:], in_=h_rows[:, m, :])
 
-        load_w(0)
+        load_w(0, WHOLE)
         load_h(0)
         load_h(1)
-        load_w(1)
+        load_w(1, WHOLE)
         load_h(2)
         load_h(3)
-        for g in range(2, PASSES):
-            load_w(g)
+        load_w(2, WHOLE)
+        for half in range(HALVES):
+            for g in range(SPLIT, PASSES):
+                load_w(g, half)
 
         h_grouped = [keep.tile([P, LAST, P, PACK], BF16, name="h_grouped%d" % m, align_bytes=64) for m in range(TOKEN_TILES)]
         h_codes = [keep.tile([P, LAST * P], U32, name="h_codes%d" % m, align_bytes=64) for m in range(TOKEN_TILES)]
@@ -107,9 +117,8 @@ def tile_feedforward_pb_kernel(tc, h, w2, ha_down, b_down, tw_down, out):
         def transpose_tile(m):
             return [transpose_bank([(m, g0 + i) for i in range(PER_BANK)]) for g0 in range(0, LAST, PER_BANK)]
 
-        def group_tile(m, banks):
-            for i, bank in enumerate(banks):
-                group_bank(nc.scalar.copy, bank, h_grouped[m][:, i * PER_BANK : (i + 1) * PER_BANK, :, :])
+        def group_part(copy, m, banks, i):
+            group_bank(copy, banks[i], h_grouped[m][:, i * PER_BANK : (i + 1) * PER_BANK, :, :])
 
         def quantise_tile(m):
             nc.vector.quantize_mx(
@@ -126,26 +135,23 @@ def tile_feedforward_pb_kernel(tc, h, w2, ha_down, b_down, tw_down, out):
                 in_=last_grouped[:, m0 : m0 + PER_BANK, :, :].rearrange("q m r t -> q (m r t)"),
             )
 
-        w_grouped = [
-            [keep.tile([P, BANK, PACK], BF16, name="w_grouped%d_%d" % (g, half), align_bytes=64) for half in range(HALVES)]
-            for g in range(PASSES)
-        ]
+        w_grouped = [keep.tile([P, N, PACK], BF16, name="w_grouped%d" % g, align_bytes=64) for g in range(PASSES)]
         w_codes = [keep.tile([P, N], U32, name="w_codes%d" % g, align_bytes=64) for g in range(PASSES)]
         w_scales = [keep.tile([P, N], U8, name="w_scales%d" % g, align_bytes=64) for g in range(PASSES)]
 
-        def regroup(g, half):
-            dst = w_grouped[g][half][:].rearrange("q (c i) t -> q c t i", i=4)
-            src = w_raw[g][:, :, half_cols(half)].rearrange("q t (c i) -> q c t i", i=4)
-            if half == LEFT:
-                nc.vector.tensor_copy(out=dst, in_=src)
-            else:
-                nc.scalar.copy(out=dst, in_=src)
+        def regroup(copy, g, first, end):
+            half = WHOLE if g < SPLIT else first // BANK
+            origin = 0 if half == WHOLE else half * BANK
+            copy(
+                out=w_grouped[g][:, first:end, :].rearrange("q (c i) t -> q c t i", i=4),
+                in_=w_raw[g, half][:, :, first - origin : end - origin].rearrange("q t (c i) -> q c t i", i=4),
+            )
 
         def quantise(g, half):
             nc.vector.quantize_mx(
                 out=w_codes[g][:, half_cols(half)].bitcast(FP8X4),
                 scales=w_scales[g][:, half_cols(half)],
-                in_=w_grouped[g][half][:].rearrange("q n t -> q (n t)"),
+                in_=w_grouped[g][:, half_cols(half), :].rearrange("q n t -> q (n t)"),
             )
 
         acc = {}
@@ -189,71 +195,92 @@ def tile_feedforward_pb_kernel(tc, h, w2, ha_down, b_down, tw_down, out):
             nc.vector.tensor_scalar(
                 out=result[m][:, half_cols(LEFT)], in0=bank[:], scalar1=gain[:, m : m + 1], scalar2=None, op0=MULT
             )
+            bank = adapter_product(m, RIGHT)
+            nc.scalar.activation(out=result[m][:, half_cols(RIGHT)], in_=bank[:], func=COPY, scale=gain[:, m : m + 1])
 
-        regroup(0, RIGHT)
-        regroup(0, LEFT)
-        quantise(0, LEFT)
-        quantise(0, RIGHT)
+        on_vector = nc.vector.tensor_copy
+        on_scalar = nc.scalar.copy
 
         tile0 = transpose_tile(0)
         tile1 = transpose_tile(1)
-        group_tile(0, tile0)
+        regroup(on_scalar, 0, BANK, N)
+        regroup(on_vector, 0, 0, BANK)
+        quantise(0, LEFT)
+        group_part(on_vector, 0, tile0, 0)
+        quantise(0, RIGHT)
+        group_part(on_scalar, 0, tile0, 1)
         last01 = transpose_bank([(0, LAST), (1, LAST)])
         quantise_tile(0)
-        group_tile(1, tile1)
-        group_bank(nc.vector.tensor_copy, last01, last_grouped[:, 0:PER_BANK, :, :])
+        group_part(on_scalar, 1, tile1, 0)
+        group_part(on_scalar, 1, tile1, 1)
+        group_bank(on_scalar, last01, last_grouped[:, 0:PER_BANK, :, :])
         quantise_tile(1)
         for m in (0, 1):
             for half in range(HALVES):
                 multiply(0, m, half)
-        regroup(1, RIGHT)
-        regroup(1, LEFT)
+        regroup(on_scalar, 1, BANK, N)
+        regroup(on_vector, 1, 0, BANK)
         quantise_last(0)
         quantise(1, LEFT)
         quantise(1, RIGHT)
 
         tile2 = transpose_tile(2)
         tile3 = transpose_tile(3)
-        group_tile(2, tile2)
+        group_part(on_vector, 2, tile2, 0)
+        group_part(on_scalar, 2, tile2, 1)
         last23 = transpose_bank([(2, LAST), (3, LAST)])
         quantise_tile(2)
-        group_tile(3, tile3)
-        group_bank(nc.vector.tensor_copy, last23, last_grouped[:, PER_BANK:, :, :])
+        group_part(on_scalar, 3, tile3, 0)
+        group_part(on_scalar, 3, tile3, 1)
+        group_bank(on_scalar, last23, last_grouped[:, PER_BANK:, :, :])
         for m in (0, 1):
             for half in range(HALVES):
                 multiply(1, m, half)
-
-        regroup(2, RIGHT)
-        regroup(2, LEFT)
+        regroup(on_scalar, 2, BANK, N)
+        regroup(on_vector, 2, 0, BANK)
         quantise_tile(3)
         quantise_last(2)
         for m in (2, 3):
             for g in (0, 1):
                 for half in range(HALVES):
                     multiply(g, m, half)
-        for g in range(2, PASSES):
-            if g > 2:
-                regroup(g, RIGHT)
-                regroup(g, LEFT)
+        for half in range(HALVES):
+            quantise(2, half)
+        for m in range(TOKEN_TILES):
             for half in range(HALVES):
-                quantise(g, half)
-                for m in range(TOKEN_TILES):
-                    multiply(g, m, half)
+                multiply(2, m, half)
 
+        for g in range(SPLIT, PASSES):
+            regroup(on_vector, g, 0, BANK // 2)
+            regroup(on_scalar, g, BANK // 2, BANK)
+        for g in range(SPLIT, PASSES):
+            quantise(g, LEFT)
         for m in range(TOKEN_TILES):
+            for g in range(SPLIT, PASSES):
+                multiply(g, m, LEFT)
+        regroup(on_scalar, SPLIT, BANK, N)
+        regroup(on_vector, LAST, VECTOR_FROM, N)
+        regroup(on_scalar, LAST, BANK, VECTOR_FROM)
+
+        def finish(m, first, end):
+            half = first // BANK
             nc.vector.tensor_tensor(
-                out=result[m][:, half_cols(LEFT)], in0=acc[m, LEFT][:], in1=result[m][:, half_cols(LEFT)], op=ADD
+                out=result[m][:, first:end],
+                in0=acc[m, half][:, first - half * BANK : end - half * BANK],
+                in1=result[m][:, first:end],
+                op=ADD,
             )
-            nc.sync.dma_start(out=out_rows[:, m, half_cols(LEFT)], in_=result[m][:, half_cols(LEFT)])
+            nc.sync.dma_start(out=out_rows[:, m, first:end], in_=result[m][:, first:end])
+
+        finish(0, 0, BANK)
+        finish(1, 0, BANK)
+        quantise(SPLIT, RIGHT)
         for m in range(TOKEN_TILES):
-            nc.scalar.copy(out=result[m][:, half_cols(RIGHT)], in_=acc[m, RIGHT][:])
-            bank = adapter_product(m, RIGHT)
-            nc.vector.scalar_tensor_tensor(
-                out=result[m][:, half_cols(RIGHT)],
-                in0=bank[:],
-                scalar=gain[:, m : m + 1],
-                in1=result[m][:, half_cols(RIGHT)],
-                op0=MULT,
-                op1=ADD,
-            )
-            nc.sync.dma_start(out=out_rows[:, m, half_cols(RIGHT)], in_=result[m][:, half_cols(RIGHT)])
+            multiply(SPLIT, m, RIGHT)
+        finish(2, 0, BANK)
+        quantise(LAST, RIGHT)
+        for m in range(TOKEN_TILES):
+            multiply(LAST, m, RIGHT)
+        finish(3, 0, BANK)
+        for m in range(TOKEN_TILES):
+            finish(m, BANK, N)

@@ -56,6 +56,11 @@ def tile_feedforward_pb_kernel(tc, h, w2, ha_down, b_down, tw_down, out):
         ident_f32 = keep.tile([P, P], F32, name="ident_f32")
         make_identity(nc, ident_f32[:])
 
+        table_in = keep.tile([P, 1], F32, name="table_in")
+        table_out = keep.tile([P, 1], F32, name="table_out")
+        nc.vector.memset(table_in[:], 0.0)
+        nc.scalar.activation(out=table_out[:], in_=table_in[:], func=COPY)
+
         ha_sb = keep.tile([P, TOKEN_TILES, R], BF16, name="ha_sb")
         nc.sync.dma_start(out=ha_sb[:], in_=ha_rows)
         b_sb = keep.tile([P, N], BF16, name="b_sb")

@@ -28,9 +28,10 @@ HALVES = N // BANK
 LEFT = 0
 RIGHT = 1
 WHOLE = 2
+WARM = 4
 SPLIT = 3
 PAIRS = 2
-VECTOR_FROM = 896
+VECTOR_FROM = 832
 PER_BANK = BANK // (PAIRS * P)
 
 FLOPS = 2 * TOKENS * K * N + 2 * TOKENS * R * N
@@ -60,6 +61,12 @@ def tile_feedforward_pb_kernel(tc, h, w2, ha_down, b_down, tw_down, out):
         table_out = keep.tile([P, 1], F32, name="table_out")
         nc.vector.memset(table_in[:], 0.0)
         nc.scalar.activation(out=table_out[:], in_=table_in[:], func=COPY)
+
+        warm = keep.tile([P, BANK], BF16, name="warm")
+        nc.vector.memset(warm[:], 0.0)
+        warm_bank = psum.tile([P, BANK], F32, name="warm_bank", tag="bank")
+        for i in range(WARM):
+            nc.tensor.matmul(out=warm_bank[:], lhsT=warm[:, 0:P], rhs=warm[:], start=True, stop=True)
 
         ha_sb = keep.tile([P, TOKEN_TILES, R], BF16, name="ha_sb")
         nc.sync.dma_start(out=ha_sb[:], in_=ha_rows)

@@ -28,6 +28,7 @@ HALVES = N // BANK
 LEFT = 0
 RIGHT = 1
 WHOLE = 2
+RUN = 8
 WARM = 4
 SPLIT = 3
 PAIRS = 2
@@ -155,8 +156,8 @@ def tile_feedforward_pb_kernel(tc, h, w2, ha_down, b_down, tw_down, out):
             half = WHOLE if g < SPLIT else first // BANK
             origin = 0 if half == WHOLE else half * BANK
             copy(
-                out=w_grouped[g][:, first:end, :].rearrange("q (c i) t -> q c t i", i=4),
-                in_=w_raw[g, half][:, :, first - origin : end - origin].rearrange("q t (c i) -> q c t i", i=4),
+                out=w_grouped[g][:, first:end, :].rearrange("q (c i) t -> q c t i", i=RUN),
+                in_=w_raw[g, half][:, :, first - origin : end - origin].rearrange("q t (c i) -> q c t i", i=RUN),
             )
 
         def quantise(g, half):

@@ -29,7 +29,7 @@ LEFT = 0
 RIGHT = 1
 WHOLE = 2
 RUN = 8
-WARM = 4
+WARM = 3
 SPLIT = 3
 PAIRS = 2
 VECTOR_FROM = 832
@@ -140,12 +140,11 @@ def tile_feedforward_pb_kernel(tc, h, w2, ha_down, b_down, tw_down, out):
                 in_=h_grouped[m][:].rearrange("q g r t -> q (g r t)"),
             )
 
-        def quantise_last(m0):
-            words = slice(m0 * P, (m0 + PER_BANK) * P)
+        def quantise_last():
             nc.vector.quantize_mx(
-                out=last_codes[:, words].bitcast(FP8X4),
-                scales=last_scales[:, words],
-                in_=last_grouped[:, m0 : m0 + PER_BANK, :, :].rearrange("q m r t -> q (m r t)"),
+                out=last_codes[:].bitcast(FP8X4),
+                scales=last_scales[:],
+                in_=last_grouped[:].rearrange("q m r t -> q (m r t)"),
             )
 
         w_grouped = [keep.tile([P, N, PACK], BF16, name="w_grouped%d" % g, align_bytes=64) for g in range(PASSES)]
@@ -218,8 +217,8 @@ def tile_feedforward_pb_kernel(tc, h, w2, ha_down, b_down, tw_down, out):
         tile1 = transpose_tile(1)
         regroup(on_scalar, 0, BANK, N)
         regroup(on_vector, 0, 0, BANK)
-        quantise(0, LEFT)
         group_part(on_vector, 0, tile0, 0)
+        quantise(0, LEFT)
         quantise(0, RIGHT)
         group_part(on_scalar, 0, tile0, 1)
         last01 = transpose_bank([(0, LAST), (1, LAST)])
@@ -227,19 +226,19 @@ def tile_feedforward_pb_kernel(tc, h, w2, ha_down, b_down, tw_down, out):
         group_part(on_scalar, 1, tile1, 0)
         group_part(on_scalar, 1, tile1, 1)
         group_bank(on_scalar, last01, last_grouped[:, 0:PER_BANK, :, :])
-        quantise_tile(1)
-        for m in (0, 1):
-            for half in range(HALVES):
-                multiply(0, m, half)
+        for half in range(HALVES):
+            multiply(0, 0, half)
         regroup(on_scalar, 1, BANK, N)
         regroup(on_vector, 1, 0, BANK)
-        quantise_last(0)
+        quantise_tile(1)
         quantise(1, LEFT)
-        quantise(1, RIGHT)
 
         tile2 = transpose_tile(2)
+        for half in range(HALVES):
+            multiply(0, 1, half)
         tile3 = transpose_tile(3)
         group_part(on_vector, 2, tile2, 0)
+        quantise(1, RIGHT)
         group_part(on_scalar, 2, tile2, 1)
         last23 = transpose_bank([(2, LAST), (3, LAST)])
         quantise_tile(2)
@@ -252,7 +251,7 @@ def tile_feedforward_pb_kernel(tc, h, w2, ha_down, b_down, tw_down, out):
         regroup(on_scalar, 2, BANK, N)
         regroup(on_vector, 2, 0, BANK)
         quantise_tile(3)
-        quantise_last(2)
+        quantise_last()
         for m in (2, 3):
             for g in (0, 1):
                 for half in range(HALVES):

@@ -40,10 +40,10 @@ FLOPS = 2 * TOKENS * K * N + 2 * TOKENS * R * N
 
 def tile_feedforward_pb_kernel(tc, h, w2, ha_down, b_down, tw_down, out):
     nc = tc.nc
-    h_rows = h.rearrange("b s k -> (b s) k").rearrange("(p m) k -> p m k", m=TOKEN_TILES)
-    ha_rows = ha_down.rearrange("b s r -> (b s) r").rearrange("(p m) r -> p m r", m=TOKEN_TILES)
-    tw_rows = tw_down.rearrange("b s -> (b s)").rearrange("(p m) -> p m", m=TOKEN_TILES)
-    out_rows = out.rearrange("b s n -> (b s) n").rearrange("(p m) n -> p m n", m=TOKEN_TILES)
+    h_rows = h.rearrange("b s k -> (b s) k").rearrange("(m p) k -> p m k", m=TOKEN_TILES)
+    ha_rows = ha_down.rearrange("b s r -> (b s) r").rearrange("(m p) r -> p m r", m=TOKEN_TILES)
+    tw_rows = tw_down.rearrange("b s -> (b s)").rearrange("(m p) -> m p", m=TOKEN_TILES)
+    out_rows = out.rearrange("b s n -> (b s) n").rearrange("(m p) n -> p m n", m=TOKEN_TILES)
 
     with ExitStack() as ctx:
         ctx.enter_context(tc.manual_schedule())
@@ -69,12 +69,14 @@ def tile_feedforward_pb_kernel(tc, h, w2, ha_down, b_down, tw_down, out):
         for i in range(WARM):
             nc.tensor.matmul(out=warm_bank[:], lhsT=warm[:, 0:P], rhs=warm[:], start=True, stop=True)
 
+        tw_sb = keep.tile([P, P], BF16, name="tw_sb")
+        nc.vector.memset(tw_sb[:], 0.0)
+
         ha_sb = keep.tile([P, TOKEN_TILES, R], BF16, name="ha_sb")
         nc.sync.dma_start(out=ha_sb[:], in_=ha_rows)
         b_sb = keep.tile([P, N], BF16, name="b_sb")
         nc.sync.dma_start(out=b_sb[:], in_=b_down)
-        tw_sb = keep.tile([P, TOKEN_TILES], BF16, name="tw_sb")
-        nc.sync.dma_start(out=tw_sb[:], in_=tw_rows)
+        nc.sync.dma_start(out=tw_sb[0:TOKEN_TILES, :], in_=tw_rows)
 
         w_raw = {}
         for g in range(PASSES):
@@ -200,7 +202,9 @@ def tile_feedforward_pb_kernel(tc, h, w2, ha_down, b_down, tw_down, out):
         for m in range(TOKEN_TILES):
             nc.tensor.transpose(ha_bank[:, m, :], ha_sb[:, m, :], ident_bf16[:])
         nc.vector.tensor_copy(out=ha_t[:], in_=ha_bank[:])
-        nc.vector.tensor_scalar(out=gain[:], in0=tw_sb[:], scalar1=SCALING, scalar2=None, op0=MULT)
+        tw_bank = psum.tile([P, P], BF16, name="tw_bank", tag="bank")
+        nc.tensor.transpose(tw_bank[:], tw_sb[:], ident_bf16[:])
+        nc.vector.tensor_scalar(out=gain[:], in0=tw_bank[:, 0:TOKEN_TILES], scalar1=SCALING, scalar2=None, op0=MULT)
 
         for m in range(TOKEN_TILES):
             bank = adapter_product(m, LEFT)
@@ -294,5 +298,7 @@ def tile_feedforward_pb_kernel(tc, h, w2, ha_down, b_down, tw_down, out):
         for m in range(TOKEN_TILES):
             multiply(LAST, m, RIGHT)
         finish(3, 0, BANK)
-        for m in range(TOKEN_TILES):
+        for m in range(TOKEN_TILES - 1):
             finish(m, BANK, N)
+        finish(TOKEN_TILES - 1, BANK, BANK + BANK // 2)
+        finish(TOKEN_TILES - 1, BANK + BANK // 2, N)

from contextlib import ExitStack

import concourse.mybir as mybir
from concourse.masks import make_identity

F32 = mybir.dt.float32
BF16 = mybir.dt.bfloat16
U32 = mybir.dt.uint32
U8 = mybir.dt.uint8
FP8X4 = mybir.dt.float8_e4m3fn_x4
MULT = mybir.AluOpType.mult
ADD = mybir.AluOpType.add
COPY = mybir.ActivationFunctionType.Copy

P = 128
PACK = 4
K_PASS = P * PACK
TOKENS = 512
K = 2560
N = 1024
R = 128
SCALING = 4.0
PASSES = K // K_PASS
LAST = PASSES - 1
TOKEN_TILES = TOKENS // P
BANK = 512
HALVES = N // BANK
LEFT = 0
RIGHT = 1
WHOLE = 2
RUN = 8
WARM = 3
SPLIT = 3
PAIRS = 2
VECTOR_FROM = 832
PER_BANK = BANK // (PAIRS * P)

FLOPS = 2 * TOKENS * K * N + 2 * TOKENS * R * N


def tile_feedforward_pb_kernel(tc, h, w2, ha_down, b_down, tw_down, out):
    nc = tc.nc
    h_rows = h.rearrange("b s k -> (b s) k").rearrange("(m p) k -> p m k", m=TOKEN_TILES)
    ha_rows = ha_down.rearrange("b s r -> (b s) r").rearrange("(m p) r -> p m r", m=TOKEN_TILES)
    tw_rows = tw_down.rearrange("b s -> (b s)").rearrange("(m p) -> m p", m=TOKEN_TILES)
    out_rows = out.rearrange("b s n -> (b s) n").rearrange("(m p) n -> p m n", m=TOKEN_TILES)

    with ExitStack() as ctx:
        ctx.enter_context(tc.manual_schedule())
        keep = ctx.enter_context(tc.tile_pool(name="keep", bufs=1))
        psum = ctx.enter_context(tc.psum_pool(name="psum", bufs=8))

        def half_cols(half):
            return slice(half * BANK, (half + 1) * BANK)

        ident_bf16 = keep.tile([P, P], BF16, name="ident_bf16")
        make_identity(nc, ident_bf16[:])
        ident_f32 = keep.tile([P, P], F32, name="ident_f32")
        make_identity(nc, ident_f32[:])

        table_in = keep.tile([P, 1], F32, name="table_in")
        table_out = keep.tile([P, 1], F32, name="table_out")
        nc.vector.memset(table_in[:], 0.0)
        nc.scalar.activation(out=table_out[:], in_=table_in[:], func=COPY)

        warm = keep.tile([P, BANK], BF16, name="warm")
        nc.vector.memset(warm[:], 0.0)
        warm_bank = psum.tile([P, BANK], F32, name="warm_bank", tag="bank")
        for i in range(WARM):
            nc.tensor.matmul(out=warm_bank[:], lhsT=warm[:, 0:P], rhs=warm[:], start=True, stop=True)

        tw_sb = keep.tile([P, P], BF16, name="tw_sb")
        nc.vector.memset(tw_sb[:], 0.0)

        ha_sb = keep.tile([P, TOKEN_TILES, R], BF16, name="ha_sb")
        nc.sync.dma_start(out=ha_sb[:], in_=ha_rows)
        b_sb = keep.tile([P, N], BF16, name="b_sb")
        nc.sync.dma_start(out=b_sb[:], in_=b_down)
        nc.sync.dma_start(out=tw_sb[0:TOKEN_TILES, :], in_=tw_rows)

        w_raw = {}
        for g in range(PASSES):
            for half in range(HALVES) if g >= SPLIT else [WHOLE]:
                w_raw[g, half] = keep.tile([P, PACK, N if half == WHOLE else BANK], BF16, name="w_raw%d_%d" % (g, half))
        h_raw = [keep.tile([P, K], BF16, name="h_raw%d" % m) for m in range(TOKEN_TILES)]

        def load_w(g, half):
            cols = slice(0, N) if half == WHOLE else half_cols(half)
            nc.sync.dma_start(
                out=w_raw[g, half][:],
                in_=w2[g * K_PASS : (g + 1) * K_PASS, cols].rearrange("(q t) n -> q t n", t=PACK),
            )

        def load_h(m):
            nc.sync.dma_start(out=h_raw[m][:], in_=h_rows[:, m, :])

        load_w(0, WHOLE)
        load_h(0)
        load_h(1)
        load_w(1, WHOLE)
        load_h(2)
        load_h(3)
        load_w(2, WHOLE)
        for half in range(HALVES):
            for g in range(SPLIT, PASSES):
                load_w(g, half)

        h_grouped = [keep.tile([P, LAST, P, PACK], BF16, name="h_grouped%d" % m, align_bytes=64) for m in range(TOKEN_TILES)]
        h_codes = [keep.tile([P, LAST * P], U32, name="h_codes%d" % m, align_bytes=64) for m in range(TOKEN_TILES)]
        h_scales = [keep.tile([P, LAST * P], U8, name="h_scales%d" % m, align_bytes=64) for m in range(TOKEN_TILES)]
        last_grouped = keep.tile([P, TOKEN_TILES, P, PACK], BF16, name="last_grouped", align_bytes=64)
        last_codes = keep.tile([P, TOKEN_TILES * P], U32, name="last_codes", align_bytes=64)
        last_scales = keep.tile([P, TOKEN_TILES * P], U8, name="last_scales", align_bytes=64)

        def transpose_bank(blocks):
            bank = psum.tile([P, PER_BANK, PAIRS, P], F32, name="h_t", tag="bank")
            for i, (m, g) in enumerate(blocks):
                words = h_raw[m][:].bitcast(F32)
                for u in range(PAIRS):
                    first = g * PAIRS * P + u
                    nc.tensor.transpose(
                        bank[:, i, u, :], words[:, first : first + PAIRS * P - u : PAIRS], ident_f32[:]
                    )
            return bank

        def group_bank(copy, bank, grouped):
            copy(
                out=grouped.rearrange("q i r t -> q i (r t)").bitcast(F32).rearrange("q i (r u) -> q i r u", u=PAIRS),
                in_=bank[:].rearrange("q i u r -> q i r u"),
            )

        def transpose_tile(m):
            return [transpose_bank([(m, g0 + i) for i in range(PER_BANK)]) for g0 in range(0, LAST, PER_BANK)]

        def group_part(copy, m, banks, i):
            group_bank(copy, banks[i], h_grouped[m][:, i * PER_BANK : (i + 1) * PER_BANK, :, :])

        def quantise_tile(m):
            nc.vector.quantize_mx(
                out=h_codes[m][:].bitcast(FP8X4),
                scales=h_scales[m][:],
                in_=h_grouped[m][:].rearrange("q g r t -> q (g r t)"),
            )

        def quantise_last():
            nc.vector.quantize_mx(
                out=last_codes[:].bitcast(FP8X4),
                scales=last_scales[:],
                in_=last_grouped[:].rearrange("q m r t -> q (m r t)"),
            )

        w_grouped = [keep.tile([P, N, PACK], BF16, name="w_grouped%d" % g, align_bytes=64) for g in range(PASSES)]
        w_codes = [keep.tile([P, N], U32, name="w_codes%d" % g, align_bytes=64) for g in range(PASSES)]
        w_scales = [keep.tile([P, N], U8, name="w_scales%d" % g, align_bytes=64) for g in range(PASSES)]

        def regroup(copy, g, first, end):
            half = WHOLE if g < SPLIT else first // BANK
            origin = 0 if half == WHOLE else half * BANK
            copy(
                out=w_grouped[g][:, first:end, :].rearrange("q (c i) t -> q c t i", i=RUN),
                in_=w_raw[g, half][:, :, first - origin : end - origin].rearrange("q t (c i) -> q c t i", i=RUN),
            )

        def quantise(g, half):
            nc.vector.quantize_mx(
                out=w_codes[g][:, half_cols(half)].bitcast(FP8X4),
                scales=w_scales[g][:, half_cols(half)],
                in_=w_grouped[g][:, half_cols(half), :].rearrange("q n t -> q (n t)"),
            )

        acc = {}

        def multiply(g, m, half):
            if g == 0:
                acc[m, half] = psum.tile([P, BANK], F32, name="acc%d_%d" % (m, half), tag="bank")
            if g == LAST:
                h_words, planes, words = last_codes, last_scales, slice(m * P, (m + 1) * P)
            else:
                h_words, planes, words = h_codes[m], h_scales[m], slice(g * P, (g + 1) * P)
            nc.tensor.matmul_mx(
                out=acc[m, half][:],
                lhsT=h_words[:, words].bitcast(FP8X4),
                lhsT_scale=planes[:, words],
                rhs=w_codes[g][:, half_cols(half)].bitcast(FP8X4),
                rhs_scale=w_scales[g][:, half_cols(half)],
                start=(g == 0),
                stop=(g == LAST),
            )

        result = [keep.tile([P, N], F32, name="result%d" % m) for m in range(TOKEN_TILES)]
        ha_t = keep.tile([P, TOKEN_TILES, P], BF16, name="ha_t")
        gain = keep.tile([P, TOKEN_TILES], F32, name="gain")

        def adapter_product(m, half):
            bank = psum.tile([P, BANK], F32, name="adapter", tag="bank")
            nc.tensor.matmul(
                out=bank[:], lhsT=ha_t[:, m, :], rhs=b_sb[:, half_cols(half)], start=True, stop=True
            )
            return bank

        ha_bank = psum.tile([P, TOKEN_TILES, P], BF16, name="ha_bank", tag="bank")
        for m in range(TOKEN_TILES):
            nc.tensor.transpose(ha_bank[:, m, :], ha_sb[:, m, :], ident_bf16[:])
        nc.vector.tensor_copy(out=ha_t[:], in_=ha_bank[:])
        tw_bank = psum.tile([P, P], BF16, name="tw_bank", tag="bank")
        nc.tensor.transpose(tw_bank[:], tw_sb[:], ident_bf16[:])
        nc.vector.tensor_scalar(out=gain[:], in0=tw_bank[:, 0:TOKEN_TILES], scalar1=SCALING, scalar2=None, op0=MULT)

        for m in range(TOKEN_TILES):
            bank = adapter_product(m, LEFT)
            nc.vector.tensor_scalar(
                out=result[m][:, half_cols(LEFT)], in0=bank[:], scalar1=gain[:, m : m + 1], scalar2=None, op0=MULT
            )
            bank = adapter_product(m, RIGHT)
            nc.scalar.activation(out=result[m][:, half_cols(RIGHT)], in_=bank[:], func=COPY, scale=gain[:, m : m + 1])

        on_vector = nc.vector.tensor_copy
        on_scalar = nc.scalar.copy

        tile0 = transpose_tile(0)
        tile1 = transpose_tile(1)
        regroup(on_scalar, 0, BANK, N)
        regroup(on_vector, 0, 0, BANK)
        group_part(on_vector, 0, tile0, 0)
        quantise(0, LEFT)
        quantise(0, RIGHT)
        group_part(on_scalar, 0, tile0, 1)
        last01 = transpose_bank([(0, LAST), (1, LAST)])
        quantise_tile(0)
        group_part(on_scalar, 1, tile1, 0)
        group_part(on_scalar, 1, tile1, 1)
        group_bank(on_scalar, last01, last_grouped[:, 0:PER_BANK, :, :])
        for half in range(HALVES):
            multiply(0, 0, half)
        regroup(on_scalar, 1, BANK, N)
        regroup(on_vector, 1, 0, BANK)
        quantise_tile(1)
        quantise(1, LEFT)

        tile2 = transpose_tile(2)
        for half in range(HALVES):
            multiply(0, 1, half)
        tile3 = transpose_tile(3)
        group_part(on_vector, 2, tile2, 0)
        quantise(1, RIGHT)
        group_part(on_scalar, 2, tile2, 1)
        last23 = transpose_bank([(2, LAST), (3, LAST)])
        quantise_tile(2)
        group_part(on_scalar, 3, tile3, 0)
        group_part(on_scalar, 3, tile3, 1)
        group_bank(on_scalar, last23, last_grouped[:, PER_BANK:, :, :])
        for m in (0, 1):
            for half in range(HALVES):
                multiply(1, m, half)
        regroup(on_scalar, 2, BANK, N)
        regroup(on_vector, 2, 0, BANK)
        quantise_tile(3)
        quantise_last()
        for m in (2, 3):
            for g in (0, 1):
                for half in range(HALVES):
                    multiply(g, m, half)
        for half in range(HALVES):
            quantise(2, half)
        for m in range(TOKEN_TILES):
            for half in range(HALVES):
                multiply(2, m, half)

        for g in range(SPLIT, PASSES):
            regroup(on_vector, g, 0, BANK // 2)
            regroup(on_scalar, g, BANK // 2, BANK)
        for g in range(SPLIT, PASSES):
            quantise(g, LEFT)
        for m in range(TOKEN_TILES):
            for g in range(SPLIT, PASSES):
                multiply(g, m, LEFT)
        regroup(on_scalar, SPLIT, BANK, N)
        regroup(on_vector, LAST, VECTOR_FROM, N)
        regroup(on_scalar, LAST, BANK, VECTOR_FROM)

        def finish(m, first, end):
            half = first // BANK
            nc.vector.tensor_tensor(
                out=result[m][:, first:end],
                in0=acc[m, half][:, first - half * BANK : end - half * BANK],
                in1=result[m][:, first:end],
                op=ADD,
            )
            nc.sync.dma_start(out=out_rows[:, m, first:end], in_=result[m][:, first:end])

        finish(0, 0, BANK)
        finish(1, 0, BANK)
        quantise(SPLIT, RIGHT)
        for m in range(TOKEN_TILES):
            multiply(SPLIT, m, RIGHT)
        finish(2, 0, BANK)
        quantise(LAST, RIGHT)
        for m in range(TOKEN_TILES):
            multiply(LAST, m, RIGHT)
        finish(3, 0, BANK)
        for m in range(TOKEN_TILES - 1):
            finish(m, BANK, N)
        finish(TOKEN_TILES - 1, BANK, BANK + BANK // 2)
        finish(TOKEN_TILES - 1, BANK + BANK // 2, N)
